import numpy as np
import ml_dtypes


def mxq(x, axis, fmt="e4m3"):
    dtype, down = {"e4m3": (ml_dtypes.float8_e4m3fn, 7), "e5m2": (ml_dtypes.float8_e5m2, 14)}[fmt]
    v = np.moveaxis(np.asarray(x, np.float32).astype(ml_dtypes.bfloat16).astype(np.float64), axis, -1)
    blocks = v.reshape(v.shape[:-1] + (-1, 32))
    amax = np.abs(blocks).max(-1, keepdims=True)
    byte = np.maximum(np.where(amax > 0, np.frexp(amax)[1] - 1 + 127, 0) - down, 1)
    scale = np.exp2(byte - 127.0)
    codes = (blocks / scale).astype(np.float32).astype(dtype).astype(np.float64)
    return np.moveaxis((codes * scale).reshape(v.shape), -1, axis)


WIDE = False


def mx_kscale(k):
    if not WIDE:
        return np.ones(k)
    levels = np.array([10, -10, 5, -5, 0])
    a = np.random.permutation(np.resize(levels, k // 512 * 4)).reshape(k // 512, 4)
    idx = np.arange(k)
    return np.exp2(a[idx // 512, idx % 128 // 32])


BF16 = ml_dtypes.bfloat16


def bf(x):
    return np.asarray(x, np.float32).astype(BF16)


def f64(x):
    return np.asarray(x).astype(np.float64)


B, In, H, Hh, E, G = 4096, 256, 256, 128, 128, 4
K = In + H
EPS = 1e-6


def rn(*shape):
    return np.random.standard_normal(shape)


def sigmoid(v):
    return 1.0 / (1.0 + np.exp(-v))


def ln(a, gamma, beta):
    mean = a.mean(-1, keepdims=True)
    std = a.std(-1, keepdims=True, ddof=1)
    return gamma * (a - mean) / (std + EPS) + beta


def setup_inputs():
    s = mx_kscale(K)
    return {
        'x': bf(rn(B, In) * s[:In]),
        'h': bf(rn(B, H) * s[In:]),
        'hyper_h': bf(rn(B, Hh)),
        'hyper_c': bf(rn(B, Hh)),
        'hc_Wih': bf(rn(G * Hh, K) / np.sqrt(K) / s[None, :]),
        'hc_bih': bf(0.3 * rn(G * Hh)),
        'hc_Whh': bf(rn(G * Hh, Hh) / np.sqrt(Hh)),
        'hc_ln_gamma': bf(1.0 + 0.1 * rn(G, Hh)),
        'hc_ln_beta': bf(0.1 * rn(G, Hh)),
        'hc_lnc_gamma': bf(1.0 + 0.1 * rn(Hh)),
        'hc_lnc_beta': bf(0.1 * rn(Hh)),
    }


def reference(x, h, hyper_h, hyper_c, hc_Wih, hc_bih, hc_Whh, hc_ln_gamma, hc_ln_beta, hc_lnc_gamma, hc_lnc_beta):
    hyper_in = np.concatenate([f64(x), f64(h)], axis=1)
    v = (mxq(hyper_in, 1, 'e4m3') @ mxq(f64(hc_Wih).T, 0, 'e4m3')) + f64(hc_bih) + f64(hyper_h) @ f64(hc_Whh).T
    v = ln(v.reshape(B, G, Hh), f64(hc_ln_gamma), f64(hc_ln_beta))
    hi, hf, hg, ho = v[:, 0], v[:, 1], v[:, 2], v[:, 3]
    hf = hf + 1.0
    new_hyper_c = f64(hyper_c) * sigmoid(hf) + sigmoid(hi) * np.tanh(hg)
    new_hyper_c = ln(new_hyper_c, f64(hc_lnc_gamma), f64(hc_lnc_beta))
    new_hyper_h = np.tanh(new_hyper_c) * sigmoid(ho)
    return new_hyper_h, new_hyper_c

@@ -1,0 +1,479 @@
+from contextlib import ExitStack
+
+import concourse.mybir as mybir
+from concourse.masks import make_identity
+
+F32 = mybir.dt.float32
+BF16 = mybir.dt.bfloat16
+U32 = mybir.dt.uint32
+U8 = mybir.dt.uint8
+FP8X4 = mybir.dt.float8_e4m3fn_x4
+ALU = mybir.AluOpType
+ACT = mybir.ActivationFunctionType
+
+P = 128
+BATCH = 4096
+IN = 256
+K = 2 * IN
+UNITS = 128
+GATES = 4
+EPS = 1e-6
+
+N_TILES = BATCH // P
+TILES_PER_GROUP = 2
+N_GROUPS = N_TILES // TILES_PER_GROUP
+GROUP_COLS = TILES_PER_GROUP * P
+GROUP_STATS = TILES_PER_GROUP * GATES
+WORDS = IN // 2
+
+GATE_FUNCS = (ACT.Sigmoid, ACT.Sigmoid, ACT.Tanh, ACT.Sigmoid)
+FORGET = 1
+OUTPUT = 3
+
+LAG = 2
+
+FLOPS = 2 * BATCH * K * GATES * UNITS + 2 * BATCH * UNITS * GATES * UNITS
+
+
+def words_to_partitions(nc, psum, ident_f32, halves, grouped):
+    k_first = psum.tile([P, 2, 2, P], F32, tag="in")
+    for i in range(2):
+        for u in range(2):
+            nc.tensor.transpose(k_first[:, i, u, :], halves[i][u], ident_f32)
+    nc.scalar.copy(
+        out=grouped.bitcast(F32).rearrange("p (i r u) -> p i r u", i=2, u=2),
+        in_=k_first[:].rearrange("p i u r -> p i r u"),
+    )
+
+
+def tile_hyperlstmcell_pa_t_kernel(
+    tc,
+    x,
+    h,
+    hyper_h,
+    hyper_c,
+    hc_Wih,
+    hc_bih,
+    hc_Whh,
+    hc_ln_gamma,
+    hc_ln_beta,
+    hc_lnc_gamma,
+    hc_lnc_beta,
+    out_0,
+    out_1,
+):
+    nc = tc.nc
+    with ExitStack() as ctx:
+        const = ctx.enter_context(tc.tile_pool(name="const", bufs=1))
+        two = ctx.enter_context(tc.tile_pool(name="two", bufs=2))
+        three = ctx.enter_context(tc.tile_pool(name="three", bufs=3))
+        four = ctx.enter_context(tc.tile_pool(name="four", bufs=4))
+        psum_in = ctx.enter_context(tc.psum_pool(name="psum_in", bufs=2))
+        psum_mx = ctx.enter_context(tc.psum_pool(name="psum_mx", bufs=2))
+        psum = ctx.enter_context(tc.psum_pool(name="psum", bufs=1))
+
+        x_rows = x.rearrange("(p r) k -> p (r k)", r=N_TILES)
+        h_rows = h.rearrange("(p r) k -> p (r k)", r=N_TILES)
+        hyper_h_rows = hyper_h.rearrange("(p r) k -> p (r k)", r=N_TILES)
+        hyper_c_rows = hyper_c.rearrange("(p r) k -> p (r k)", r=N_TILES)
+        new_h_rows = out_0.rearrange("(p r) k -> p (r k)", r=N_TILES)
+        new_c_rows = out_1.rearrange("(p r) k -> p (r k)", r=N_TILES)
+
+        kept_tiles = [dict() for group in range(N_GROUPS)]
+
+        def outside(group):
+            return group < 0 or group >= N_GROUPS
+
+        def load(group):
+            if outside(group):
+                return
+            x_sb = four.tile([P, TILES_PER_GROUP * IN], BF16)
+            h_sb = four.tile([P, TILES_PER_GROUP * IN], BF16)
+            hyper_h_sb = four.tile([P, GROUP_COLS], BF16)
+            hyper_c_sb = four.tile([P, GROUP_COLS], BF16)
+            wide = slice(group * TILES_PER_GROUP * IN, (group + 1) * TILES_PER_GROUP * IN)
+            narrow = slice(group * GROUP_COLS, (group + 1) * GROUP_COLS)
+            nc.sync.dma_start(out=x_sb[:], in_=x_rows[:, wide])
+            nc.sync.dma_start(out=h_sb[:], in_=h_rows[:, wide])
+            nc.sync.dma_start(out=hyper_h_sb[:], in_=hyper_h_rows[:, narrow])
+            nc.sync.dma_start(out=hyper_c_sb[:], in_=hyper_c_rows[:, narrow])
+            kept_tiles[group]["x_sb"] = x_sb
+            kept_tiles[group]["h_sb"] = h_sb
+            kept_tiles[group]["hyper_h_sb"] = hyper_h_sb
+            kept_tiles[group]["hyper_c_sb"] = hyper_c_sb
+
+        wih_rows = const.tile([P, GATES * K], BF16)
+        nc.sync.dma_start(
+            out=wih_rows[:].rearrange("p (g k) -> p g k", g=GATES),
+            in_=hc_Wih.rearrange("(g p) k -> p g k", p=P),
+        )
+        load(0)
+        load(1)
+
+        ident_f32 = const.tile([P, P], F32)
+        make_identity(nc, ident_f32[:])
+        ident_bf16 = const.tile([P, P], BF16)
+        make_identity(nc, ident_bf16[:])
+
+        wih_words = wih_rows[:].bitcast(F32)
+        wih_grouped = const.tile([P, GATES * P * 4], BF16, align_bytes=64)
+        wih_codes = const.tile([P, GATES * P], U32, align_bytes=64)
+        wih_scales = const.tile([P, GATES * P], U8, align_bytes=64)
+        for pair in range(GATES // 2):
+            words_to_partitions(
+                nc,
+                psum_in,
+                ident_f32[:],
+                [
+                    (
+                        wih_words[:, 2 * g * WORDS : (2 * g + 1) * WORDS],
+                        wih_words[:, (2 * g + 1) * WORDS : (2 * g + 2) * WORDS],
+                    )
+                    for g in (2 * pair, 2 * pair + 1)
+                ],
+                wih_grouped[:, 2 * pair * P * 4 : (2 * pair + 2) * P * 4],
+            )
+        nc.vector.quantize_mx(out=wih_codes[:].bitcast(FP8X4), scales=wih_scales[:], in_=wih_grouped[:])
+
+        whh_rows = const.tile([P, GATES * UNITS], BF16)
+        nc.scalar.dma_start(
+            out=whh_rows[:].rearrange("p (g k) -> p g k", g=GATES),
+            in_=hc_Whh.rearrange("(g p) k -> p g k", p=P),
+        )
+        whh_t_ps = psum_in.tile([P, GATES * P], BF16, tag="in")
+        for g in range(GATES):
+            nc.tensor.transpose(
+                whh_t_ps[:, g * P : (g + 1) * P], whh_rows[:, g * UNITS : (g + 1) * UNITS], ident_bf16[:]
+            )
+        whh_t = const.tile([P, GATES * P], BF16)
+        nc.vector.tensor_copy(out=whh_t[:], in_=whh_t_ps[:])
+
+        bias_all = const.tile([P, GATES, UNITS], BF16)
+        nc.scalar.dma_start(out=bias_all[:].rearrange("p g j -> p (g j)"), in_=hc_bih.partition_broadcast(P))
+        gamma_c_all = const.tile([P, UNITS], BF16)
+        nc.scalar.dma_start(out=gamma_c_all[:], in_=hc_lnc_gamma.partition_broadcast(P))
+        beta_c_all = const.tile([P, UNITS], BF16)
+        nc.scalar.dma_start(out=beta_c_all[:], in_=hc_lnc_beta.partition_broadcast(P))
+
+        gate_rows = const.tile([P, P], BF16)
+        nc.vector.memset(gate_rows[:], 0.0)
+        nc.scalar.dma_start(out=gate_rows[0:GATES, :], in_=hc_ln_gamma)
+        nc.scalar.dma_start(out=gate_rows[GATES : 2 * GATES, :], in_=hc_ln_beta)
+        gate_cols_ps = psum_in.tile([P, P], BF16, tag="in")
+        nc.tensor.transpose(gate_cols_ps[:], gate_rows[:], ident_bf16[:])
+        gate_cols = const.tile([P, 2 * GATES], F32)
+        nc.vector.tensor_copy(out=gate_cols[:], in_=gate_cols_ps[:, 0 : 2 * GATES])
+        forget_beta = gate_cols[:, GATES + FORGET : GATES + FORGET + 1]
+        nc.vector.tensor_scalar_add(out=forget_beta, in0=forget_beta, scalar1=1.0)
+
+        half = const.tile([P, GROUP_STATS], F32)
+        nc.vector.memset(half[:], 0.5)
+
+        def transpose_inputs(group):
+            if outside(group):
+                return
+            kept = kept_tiles[group]
+            x_words = kept["x_sb"][:].bitcast(F32)
+            h_words = kept["h_sb"][:].bitcast(F32)
+            u_grouped = two.tile([P, GROUP_COLS * 4], BF16, align_bytes=64)
+            words_to_partitions(
+                nc,
+                psum_in,
+                ident_f32[:],
+                [
+                    (x_words[:, t * WORDS : (t + 1) * WORDS], h_words[:, t * WORDS : (t + 1) * WORDS])
+                    for t in range(TILES_PER_GROUP)
+                ],
+                u_grouped[:],
+            )
+            state_t_ps = psum_in.tile([P, 2, GROUP_COLS], BF16, tag="in")
+            for t in range(TILES_PER_GROUP):
+                cols = slice(t * P, (t + 1) * P)
+                nc.tensor.transpose(state_t_ps[:, 0, cols], kept["hyper_h_sb"][:, cols], ident_bf16[:])
+                nc.tensor.transpose(state_t_ps[:, 1, cols], kept["hyper_c_sb"][:, cols], ident_bf16[:])
+            state_t = four.tile([P, 2, GROUP_COLS], BF16)
+            nc.scalar.copy(out=state_t[:], in_=state_t_ps[:])
+            kept["u_grouped"] = u_grouped
+            kept["hyper_h_t"] = state_t[:, 0, :]
+            kept["hyper_c_t"] = state_t[:, 1, :]
+
+        def quantise(group):
+            if outside(group):
+                return
+            kept = kept_tiles[group]
+            u_codes = two.tile([P, GROUP_COLS], U32, align_bytes=64)
+            u_scales = two.tile([P, GROUP_COLS], U8, align_bytes=64)
+            nc.vector.quantize_mx(out=u_codes[:].bitcast(FP8X4), scales=u_scales[:], in_=kept["u_grouped"][:])
+            kept["u_codes"] = u_codes
+            kept["u_scales"] = u_scales
+
+        def products(group, t):
+            if outside(group):
+                return
+            kept = kept_tiles[group]
+            cols = slice(t * P, (t + 1) * P)
+            mx = psum_mx.tile([P, GATES, UNITS], F32)
+            nc.tensor.matmul_mx(
+                out=mx[:].rearrange("p g j -> p (g j)"),
+                lhsT=kept["u_codes"][:, cols].bitcast(FP8X4),
+                lhsT_scale=kept["u_scales"][:, cols],
+                rhs=wih_codes[:].bitcast(FP8X4),
+                rhs_scale=wih_scales[:],
+                start=True,
+                stop=True,
+            )
+            plain = psum.tile([P, GATES, UNITS], F32, tag="plain")
+            nc.tensor.matmul(
+                out=plain[:].rearrange("p g j -> p (g j)"),
+                lhsT=kept["hyper_h_t"][:, cols],
+                rhs=whh_t[:],
+                start=True,
+                stop=True,
+            )
+            kept["mx", t] = mx
+            kept["plain", t] = plain
+
+        def add_and_sum(group, t):
+            if outside(group):
+                return
+            kept = kept_tiles[group]
+            if t == 0:
+                v = three.tile([P, TILES_PER_GROUP, GATES, UNITS], F32)
+                v_sum = three.tile([P, GROUP_STATS], F32)
+                sum_sq = three.tile([P, GROUP_STATS], F32)
+                squares = const.tile([P, TILES_PER_GROUP, GATES, UNITS], F32)
+                kept["v"] = v
+                kept["v_sum"] = v_sum
+                kept["sum_sq"] = sum_sq
+                kept["squares"] = squares
+            mx, plain, v, v_sum = kept["mx", t], kept["plain", t], kept["v"], kept["v_sum"]
+            plain_bias = two.tile([P, GATES, UNITS], F32)
+            for step in range(GATES + LAG):
+                if step < GATES:
+                    nc.vector.tensor_tensor(
+                        out=plain_bias[:, step, :], in0=plain[:, step, :], in1=bias_all[:, step, :], op=ALU.add
+                    )
+                if step >= LAG:
+                    g = step - LAG
+                    nc.vector.scalar_tensor_tensor(
+                        out=v[:, t, g, :],
+                        in0=mx[:, g, :],
+                        scalar=1.0,
+                        in1=plain_bias[:, g, :],
+                        op0=ALU.mult,
+                        op1=ALU.add,
+                        accum_out=v_sum[:, t * GATES + g : t * GATES + g + 1],
+                    )
+            for g in range(GATES):
+                col = slice(t * GATES + g, t * GATES + g + 1)
+                nc.scalar.activation(
+                    out=kept["squares"][:, t, g, :],
+                    in_=v[:, t, g, :],
+                    func=ACT.Square,
+                    bias=v_sum[:, col],
+                    scale=-float(UNITS),
+                    accum_out=kept["sum_sq"][:, col],
+                )
+
+        def gate_roots(group):
+            if outside(group):
+                return
+            kept = kept_tiles[group]
+            root = three.tile([P, GROUP_STATS], F32)
+            nc.gpsimd.tensor_tensor(out=root[:], in0=kept["sum_sq"][:], in1=half[:], op=ALU.pow)
+            kept["root"] = root
+
+        def gate_std(group):
+            if outside(group):
+                return
+            kept = kept_tiles[group]
+            std_eps = two.tile([P, GROUP_STATS], F32)
+            nc.vector.tensor_scalar(
+                out=std_eps[:],
+                in0=kept["root"][:],
+                scalar1=1.0 / (UNITS * (UNITS - 1) ** 0.5),
+                scalar2=EPS,
+                op0=ALU.mult,
+                op1=ALU.add,
+            )
+            neg_mean = two.tile([P, GROUP_STATS], F32)
+            nc.vector.tensor_scalar_mul(out=neg_mean[:], in0=kept["v_sum"][:], scalar1=-1.0 / UNITS)
+            kept["std_eps"] = std_eps
+            kept["neg_mean"] = neg_mean
+
+        def gate_inv_std(group):
+            if outside(group):
+                return
+            kept = kept_tiles[group]
+            inv_std = two.tile([P, GROUP_STATS], F32)
+            nc.vector.reciprocal(out=inv_std[:], in_=kept["std_eps"][:])
+            kept["inv_std"] = inv_std
+
+        def normalise(group):
+            if outside(group):
+                return
+            kept = kept_tiles[group]
+            normed = two.tile([P, TILES_PER_GROUP, GATES, UNITS], F32)
+            for t in range(TILES_PER_GROUP):
+                for g in range(GATES):
+                    col = slice(t * GATES + g, t * GATES + g + 1)
+                    nc.vector.tensor_scalar(
+                        out=normed[:, t, g, :],
+                        in0=kept["v"][:, t, g, :],
+                        scalar1=kept["neg_mean"][:, col],
+                        scalar2=kept["inv_std"][:, col],
+                        op0=ALU.add,
+                        op1=ALU.mult,
+                    )
+            norm_if = psum.tile([P, 2, TILES_PER_GROUP, P], F32, tag="norm_if")
+            norm_go = psum.tile([P, 2, TILES_PER_GROUP, P], F32, tag="norm_go")
+            banks = (norm_if, norm_go)
+            for t in range(TILES_PER_GROUP):
+                for g in range(GATES):
+                    nc.tensor.transpose(banks[g // 2][:, g % 2, t, :], normed[:, t, g, :], ident_f32[:])
+            gate_i = three.tile([P, GROUP_COLS], F32)
+            gate_f = three.tile([P, GROUP_COLS], F32)
+            gate_g = three.tile([P, GROUP_COLS], F32)
+            gate_o = three.tile([P, GROUP_COLS], F32)
+            gates = (gate_i, gate_f, gate_g, gate_o)
+            for g in range(GATES):
+                nc.scalar.activation(
+                    out=gates[g][:],
+                    in_=banks[g // 2][:, g % 2, :, :].rearrange("p t b -> p (t b)"),
+                    func=GATE_FUNCS[g],
+                    scale=gate_cols[:, g : g + 1],
+                    bias=gate_cols[:, GATES + g : GATES + g + 1],
+                )
+            kept["gates"] = gates
+
+        def cell_product(group):
+            if outside(group):
+                return
+            kept = kept_tiles[group]
+            gate_i, gate_f, gate_g, gate_o = kept["gates"]
+            old_part = two.tile([P, GROUP_COLS], F32)
+            nc.gpsimd.tensor_tensor(out=old_part[:], in0=gate_f[:], in1=kept["hyper_c_t"], op=ALU.mult)
+            new_part = two.tile([P, GROUP_COLS], F32)
+            nc.gpsimd.tensor_tensor(out=new_part[:], in0=gate_i[:], in1=gate_g[:], op=ALU.mult)
+            raw_c = three.tile([P, GROUP_COLS], F32)
+            nc.gpsimd.tensor_tensor(out=raw_c[:], in0=old_part[:], in1=new_part[:], op=ALU.add)
+            kept["raw_c"] = raw_c
+
+        def transpose_back(group):
+            if outside(group):
+                return
+            kept = kept_tiles[group]
+            back = psum.tile([P, 2, TILES_PER_GROUP, UNITS], F32, tag="back")
+            for t in range(TILES_PER_GROUP):
+                cols = slice(t * P, (t + 1) * P)
+                nc.tensor.transpose(back[:, 0, t, :], kept["raw_c"][:, cols], ident_f32[:])
+                nc.tensor.transpose(back[:, 1, t, :], kept["gates"][OUTPUT][:, cols], ident_f32[:])
+            gate_o_rows = three.tile([P, TILES_PER_GROUP, UNITS], F32)
+            nc.scalar.copy(out=gate_o_rows[:], in_=back[:, 1, :, :])
+            kept["back"] = back
+            kept["gate_o_rows"] = gate_o_rows
+
+        def cell_stats(group):
+            if outside(group):
+                return
+            kept = kept_tiles[group]
+            raw_c_rows = kept["back"][:, 0, :, :]
+            c_stats = two.tile([P, TILES_PER_GROUP, 6], F32)
+            c_mean_var = three.tile([P, TILES_PER_GROUP, 2], F32)
+            for t in range(TILES_PER_GROUP):
+                nc.vector.bn_stats(out=c_stats[:, t, :], in_=raw_c_rows[:, t, :])
+            for t in range(TILES_PER_GROUP):
+                nc.vector.bn_aggr(out=c_mean_var[:, t, :], in_=c_stats[:, t, :])
+            centred = two.tile([P, TILES_PER_GROUP, UNITS], F32)
+            for t in range(TILES_PER_GROUP):
+                nc.vector.scalar_tensor_tensor(
+                    out=centred[:, t, :],
+                    in0=raw_c_rows[:, t, :],
+                    scalar=c_mean_var[:, t, 0:1],
+                    in1=gamma_c_all[:],
+                    op0=ALU.subtract,
+                    op1=ALU.mult,
+                )
+            c_root = three.tile([P, TILES_PER_GROUP], F32)
+            nc.gpsimd.tensor_tensor(
+                out=c_root[:], in0=c_mean_var[:, :, 1], in1=half[:, 0:TILES_PER_GROUP], op=ALU.pow
+            )
+            kept["centred"] = centred
+            kept["c_root"] = c_root
+
+        def cell_std(group):
+            if outside(group):
+                return
+            kept = kept_tiles[group]
+            c_std_eps = two.tile([P, TILES_PER_GROUP], F32)
+            nc.vector.tensor_scalar(
+                out=c_std_eps[:],
+                in0=kept["c_root"][:],
+                scalar1=(UNITS / (UNITS - 1)) ** 0.5,
+                scalar2=EPS,
+                op0=ALU.mult,
+                op1=ALU.add,
+            )
+            kept["c_std_eps"] = c_std_eps
+
+        def cell_inv_std(group):
+            if outside(group):
+                return
+            kept = kept_tiles[group]
+            c_inv_std = two.tile([P, TILES_PER_GROUP], F32)
+            nc.vector.reciprocal(out=c_inv_std[:], in_=kept["c_std_eps"][:])
+            kept["c_inv_std"] = c_inv_std
+
+        def cell_out(group):
+            if outside(group):
+                return
+            kept = kept_tiles[group]
+            new_c = three.tile([P, TILES_PER_GROUP, UNITS], F32)
+            for t in range(TILES_PER_GROUP):
+                nc.vector.scalar_tensor_tensor(
+                    out=new_c[:, t, :],
+                    in0=kept["centred"][:, t, :],
+                    scalar=kept["c_inv_std"][:, t : t + 1],
+                    in1=beta_c_all[:],
+                    op0=ALU.mult,
+                    op1=ALU.add,
+                )
+            new_c_flat = new_c[:].rearrange("p t j -> p (t j)")
+            nc.sync.dma_start(out=new_c_rows[:, group * GROUP_COLS : (group + 1) * GROUP_COLS], in_=new_c_flat)
+            tanh_c = two.tile([P, GROUP_COLS], F32)
+            nc.scalar.activation(out=tanh_c[:], in_=new_c_flat, func=ACT.Tanh)
+            kept["tanh_c"] = tanh_c
+
+        def hidden_out(group):
+            if outside(group):
+                return
+            kept = kept_tiles[group]
+            new_h = three.tile([P, GROUP_COLS], F32)
+            nc.vector.tensor_tensor(
+                out=new_h[:],
+                in0=kept["gate_o_rows"][:].rearrange("p t j -> p (t j)"),
+                in1=kept["tanh_c"][:],
+                op=ALU.mult,
+            )
+            nc.sync.dma_start(out=new_h_rows[:, group * GROUP_COLS : (group + 1) * GROUP_COLS], in_=new_h[:])
+
+        with tc.manual_schedule():
+            for i in range(-2, N_GROUPS + 5):
+                load(i + 4)
+                products(i, 1)
+                transpose_back(i - 3)
+                add_and_sum(i, 0)
+                gate_std(i - 1)
+                cell_std(i - 4)
+                hidden_out(i - 5)
+                gate_inv_std(i - 1)
+                cell_inv_std(i - 4)
+                quantise(i + 1)
+                add_and_sum(i, 1)
+                gate_roots(i)
+                transpose_inputs(i + 2)
+                products(i + 1, 0)
+                normalise(i - 1)
+                cell_out(i - 4)
+                cell_stats(i - 3)
+                cell_product(i - 1)

@@ -463,14 +463,14 @@ def tile_hyperlstmcell_pa_t_kernel(
                 products(i, 1)
                 transpose_back(i - 3)
                 add_and_sum(i, 0)
+                add_and_sum(i, 1)
+                gate_roots(i)
                 gate_std(i - 1)
                 cell_std(i - 4)
                 hidden_out(i - 5)
                 gate_inv_std(i - 1)
                 cell_inv_std(i - 4)
                 quantise(i + 1)
-                add_and_sum(i, 1)
-                gate_roots(i)
                 transpose_inputs(i + 2)
                 products(i + 1, 0)
                 normalise(i - 1)

@@ -352,11 +352,11 @@ def tile_hyperlstmcell_pa_t_kernel(
             kept = kept_tiles[group]
             gate_i, gate_f, gate_g, gate_o = kept["gates"]
             old_part = two.tile([P, GROUP_COLS], F32)
-            nc.gpsimd.tensor_tensor(out=old_part[:], in0=gate_f[:], in1=kept["hyper_c_t"], op=ALU.mult)
+            nc.vector.tensor_tensor(out=old_part[:], in0=gate_f[:], in1=kept["hyper_c_t"], op=ALU.mult)
             new_part = two.tile([P, GROUP_COLS], F32)
-            nc.gpsimd.tensor_tensor(out=new_part[:], in0=gate_i[:], in1=gate_g[:], op=ALU.mult)
+            nc.vector.tensor_tensor(out=new_part[:], in0=gate_i[:], in1=gate_g[:], op=ALU.mult)
             raw_c = three.tile([P, GROUP_COLS], F32)
-            nc.gpsimd.tensor_tensor(out=raw_c[:], in0=old_part[:], in1=new_part[:], op=ALU.add)
+            nc.vector.tensor_tensor(out=raw_c[:], in0=old_part[:], in1=new_part[:], op=ALU.add)
             kept["raw_c"] = raw_c
 
         def transpose_back(group):
@@ -471,9 +471,9 @@ def tile_hyperlstmcell_pa_t_kernel(
                 gate_inv_std(i - 1)
                 cell_inv_std(i - 4)
                 quantise(i + 1)
+                cell_product(i - 2)
                 transpose_inputs(i + 2)
                 products(i + 1, 0)
                 normalise(i - 1)
                 cell_out(i - 4)
                 cell_stats(i - 3)
-                cell_product(i - 1)

@@ -296,10 +296,7 @@ def tile_hyperlstmcell_pa_t_kernel(
                 op0=ALU.mult,
                 op1=ALU.add,
             )
-            neg_mean = two.tile([P, GROUP_STATS], F32)
-            nc.vector.tensor_scalar_mul(out=neg_mean[:], in0=kept["v_sum"][:], scalar1=-1.0 / UNITS)
             kept["std_eps"] = std_eps
-            kept["neg_mean"] = neg_mean
 
         def gate_inv_std(group):
             if outside(group):
@@ -309,6 +306,21 @@ def tile_hyperlstmcell_pa_t_kernel(
             nc.vector.reciprocal(out=inv_std[:], in_=kept["std_eps"][:])
             kept["inv_std"] = inv_std
 
+        def gate_shift(group):
+            if outside(group):
+                return
+            kept = kept_tiles[group]
+            shift = two.tile([P, GROUP_STATS], F32)
+            nc.vector.scalar_tensor_tensor(
+                out=shift[:],
+                in0=kept["v_sum"][:],
+                scalar=-1.0 / UNITS,
+                in1=kept["inv_std"][:],
+                op0=ALU.mult,
+                op1=ALU.mult,
+            )
+            kept["shift"] = shift
+
         def normalise(group):
             if outside(group):
                 return
@@ -317,20 +329,32 @@ def tile_hyperlstmcell_pa_t_kernel(
             for t in range(TILES_PER_GROUP):
                 for g in range(GATES):
                     col = slice(t * GATES + g, t * GATES + g + 1)
-                    nc.vector.tensor_scalar(
+                    nc.scalar.activation(
                         out=normed[:, t, g, :],
-                        in0=kept["v"][:, t, g, :],
-                        scalar1=kept["neg_mean"][:, col],
-                        scalar2=kept["inv_std"][:, col],
-                        op0=ALU.add,
-                        op1=ALU.mult,
+                        in_=kept["v"][:, t, g, :],
+                        func=ACT.Identity,
+                        scale=kept["inv_std"][:, col],
+                        bias=kept["shift"][:, col],
                     )
+            kept["normed"] = normed
+
+        def transpose_normed(group):
+            if outside(group):
+                return
+            kept = kept_tiles[group]
             norm_if = psum.tile([P, 2, TILES_PER_GROUP, P], F32, tag="norm_if")
             norm_go = psum.tile([P, 2, TILES_PER_GROUP, P], F32, tag="norm_go")
             banks = (norm_if, norm_go)
             for t in range(TILES_PER_GROUP):
                 for g in range(GATES):
-                    nc.tensor.transpose(banks[g // 2][:, g % 2, t, :], normed[:, t, g, :], ident_f32[:])
+                    nc.tensor.transpose(banks[g // 2][:, g % 2, t, :], kept["normed"][:, t, g, :], ident_f32[:])
+            kept["banks"] = banks
+
+        def activate(group):
+            if outside(group):
+                return
+            kept = kept_tiles[group]
+            banks = kept["banks"]
             gate_i = three.tile([P, GROUP_COLS], F32)
             gate_f = three.tile([P, GROUP_COLS], F32)
             gate_g = three.tile([P, GROUP_COLS], F32)
@@ -471,9 +495,12 @@ def tile_hyperlstmcell_pa_t_kernel(
                 gate_inv_std(i - 1)
                 cell_inv_std(i - 4)
                 quantise(i + 1)
+                gate_shift(i - 1)
                 cell_product(i - 2)
+                normalise(i - 1)
                 transpose_inputs(i + 2)
                 products(i + 1, 0)
-                normalise(i - 1)
+                transpose_normed(i - 1)
                 cell_out(i - 4)
+                activate(i - 1)
                 cell_stats(i - 3)

@@ -30,16 +30,23 @@ GATE_FUNCS = (ACT.Sigmoid, ACT.Sigmoid, ACT.Tanh, ACT.Sigmoid)
 FORGET = 1
 OUTPUT = 3
 
-LAG = 2
+CELL_LAG = 3
+ROUND_STATS = GROUP_STATS + TILES_PER_GROUP
+
+LOADS_AHEAD = 4
 
 FLOPS = 2 * BATCH * K * GATES * UNITS + 2 * BATCH * UNITS * GATES * UNITS
 
 
-def words_to_partitions(nc, psum, ident_f32, halves, grouped):
+def transpose_words(nc, psum, ident_f32, halves):
     k_first = psum.tile([P, 2, 2, P], F32, tag="in")
     for i in range(2):
         for u in range(2):
             nc.tensor.transpose(k_first[:, i, u, :], halves[i][u], ident_f32)
+    return k_first
+
+
+def group_words(nc, k_first, grouped):
     nc.scalar.copy(
         out=grouped.bitcast(F32).rearrange("p (i r u) -> p i r u", i=2, u=2),
         in_=k_first[:].rearrange("p i u r -> p i r u"),
@@ -65,9 +72,7 @@ def tile_hyperlstmcell_pa_t_kernel(
     nc = tc.nc
     with ExitStack() as ctx:
         const = ctx.enter_context(tc.tile_pool(name="const", bufs=1))
-        two = ctx.enter_context(tc.tile_pool(name="two", bufs=2))
-        three = ctx.enter_context(tc.tile_pool(name="three", bufs=3))
-        four = ctx.enter_context(tc.tile_pool(name="four", bufs=4))
+        work = ctx.enter_context(tc.tile_pool(name="work", bufs=2))
         psum_in = ctx.enter_context(tc.psum_pool(name="psum_in", bufs=2))
         psum_mx = ctx.enter_context(tc.psum_pool(name="psum_mx", bufs=2))
         psum = ctx.enter_context(tc.psum_pool(name="psum", bufs=1))
@@ -80,17 +85,23 @@ def tile_hyperlstmcell_pa_t_kernel(
         new_c_rows = out_1.rearrange("(p r) k -> p (r k)", r=N_TILES)
 
         kept_tiles = [dict() for group in range(N_GROUPS)]
+        shared_tiles = [dict() for r in range(N_GROUPS + CELL_LAG)]
 
         def outside(group):
             return group < 0 or group >= N_GROUPS
 
+        def live_columns(r):
+            first = 0 if r < N_GROUPS else GROUP_STATS
+            last = ROUND_STATS if r >= CELL_LAG else GROUP_STATS
+            return slice(first, last)
+
         def load(group):
             if outside(group):
                 return
-            x_sb = four.tile([P, TILES_PER_GROUP * IN], BF16)
-            h_sb = four.tile([P, TILES_PER_GROUP * IN], BF16)
-            hyper_h_sb = four.tile([P, GROUP_COLS], BF16)
-            hyper_c_sb = four.tile([P, GROUP_COLS], BF16)
+            x_sb = work.tile([P, TILES_PER_GROUP * IN], BF16, bufs=LOADS_AHEAD)
+            h_sb = work.tile([P, TILES_PER_GROUP * IN], BF16, bufs=LOADS_AHEAD)
+            hyper_h_sb = work.tile([P, GROUP_COLS], BF16, bufs=LOADS_AHEAD)
+            hyper_c_sb = work.tile([P, GROUP_COLS], BF16, bufs=LOADS_AHEAD)
             wide = slice(group * TILES_PER_GROUP * IN, (group + 1) * TILES_PER_GROUP * IN)
             narrow = slice(group * GROUP_COLS, (group + 1) * GROUP_COLS)
             nc.sync.dma_start(out=x_sb[:], in_=x_rows[:, wide])
@@ -120,7 +131,7 @@ def tile_hyperlstmcell_pa_t_kernel(
         wih_codes = const.tile([P, GATES * P], U32, align_bytes=64)
         wih_scales = const.tile([P, GATES * P], U8, align_bytes=64)
         for pair in range(GATES // 2):
-            words_to_partitions(
+            wih_t_ps = transpose_words(
                 nc,
                 psum_in,
                 ident_f32[:],
@@ -131,8 +142,8 @@ def tile_hyperlstmcell_pa_t_kernel(
                     )
                     for g in (2 * pair, 2 * pair + 1)
                 ],
-                wih_grouped[:, 2 * pair * P * 4 : (2 * pair + 2) * P * 4],
             )
+            group_words(nc, wih_t_ps, wih_grouped[:, 2 * pair * P * 4 : (2 * pair + 2) * P * 4])
         nc.vector.quantize_mx(out=wih_codes[:].bitcast(FP8X4), scales=wih_scales[:], in_=wih_grouped[:])
 
         whh_rows = const.tile([P, GATES * UNITS], BF16)
@@ -148,12 +159,39 @@ def tile_hyperlstmcell_pa_t_kernel(
         whh_t = const.tile([P, GATES * P], BF16)
         nc.vector.tensor_copy(out=whh_t[:], in_=whh_t_ps[:])
 
+        vector_rows = const.tile([P, (GATES + 2) * UNITS], BF16)
+        nc.vector.memset(vector_rows[:], 0.0)
+        nc.scalar.dma_start(out=vector_rows[0:1, 0 : GATES * UNITS], in_=hc_bih.rearrange("(o n) -> o n", o=1))
+        nc.scalar.dma_start(
+            out=vector_rows[0:1, GATES * UNITS : (GATES + 1) * UNITS], in_=hc_lnc_gamma.rearrange("(o n) -> o n", o=1)
+        )
+        nc.scalar.dma_start(
+            out=vector_rows[0:1, (GATES + 1) * UNITS : (GATES + 2) * UNITS], in_=hc_lnc_beta.rearrange("(o n) -> o n", o=1)
+        )
+        ones = const.tile([P, P], BF16)
+        nc.vector.memset(ones[:], 1.0)
+        bias_ps = psum_in.tile([P, GATES, UNITS], F32, tag="in")
+        nc.tensor.matmul(
+            out=bias_ps[:].rearrange("p g j -> p (g j)"),
+            lhsT=ones[:],
+            rhs=vector_rows[:, 0 : GATES * UNITS],
+            start=True,
+            stop=True,
+        )
         bias_all = const.tile([P, GATES, UNITS], BF16)
-        nc.scalar.dma_start(out=bias_all[:].rearrange("p g j -> p (g j)"), in_=hc_bih.partition_broadcast(P))
-        gamma_c_all = const.tile([P, UNITS], BF16)
-        nc.scalar.dma_start(out=gamma_c_all[:], in_=hc_lnc_gamma.partition_broadcast(P))
-        beta_c_all = const.tile([P, UNITS], BF16)
-        nc.scalar.dma_start(out=beta_c_all[:], in_=hc_lnc_beta.partition_broadcast(P))
+        nc.vector.tensor_copy(out=bias_all[:], in_=bias_ps[:])
+        cell_ps = psum_in.tile([P, 2, UNITS], F32, tag="in")
+        nc.tensor.matmul(
+            out=cell_ps[:].rearrange("p c j -> p (c j)"),
+            lhsT=ones[:],
+            rhs=vector_rows[:, GATES * UNITS : (GATES + 2) * UNITS],
+            start=True,
+            stop=True,
+        )
+        cell_all = const.tile([P, 2, UNITS], BF16)
+        nc.vector.tensor_copy(out=cell_all[:], in_=cell_ps[:])
+        gamma_c_all = cell_all[:, 0, :]
+        beta_c_all = cell_all[:, 1, :]
 
         gate_rows = const.tile([P, P], BF16)
         nc.vector.memset(gate_rows[:], 0.0)
@@ -166,8 +204,10 @@ def tile_hyperlstmcell_pa_t_kernel(
         forget_beta = gate_cols[:, GATES + FORGET : GATES + FORGET + 1]
         nc.vector.tensor_scalar_add(out=forget_beta, in0=forget_beta, scalar1=1.0)
 
-        half = const.tile([P, GROUP_STATS], F32)
+        half = const.tile([P, ROUND_STATS], F32)
         nc.vector.memset(half[:], 0.5)
+
+        squares = const.tile([P, TILES_PER_GROUP, GATES, UNITS], F32)
 
         def transpose_inputs(group):
             if outside(group):
@@ -175,8 +215,7 @@ def tile_hyperlstmcell_pa_t_kernel(
             kept = kept_tiles[group]
             x_words = kept["x_sb"][:].bitcast(F32)
             h_words = kept["h_sb"][:].bitcast(F32)
-            u_grouped = two.tile([P, GROUP_COLS * 4], BF16, align_bytes=64)
-            words_to_partitions(
+            kept["u_t_ps"] = transpose_words(
                 nc,
                 psum_in,
                 ident_f32[:],
@@ -184,15 +223,22 @@ def tile_hyperlstmcell_pa_t_kernel(
                     (x_words[:, t * WORDS : (t + 1) * WORDS], h_words[:, t * WORDS : (t + 1) * WORDS])
                     for t in range(TILES_PER_GROUP)
                 ],
-                u_grouped[:],
             )
             state_t_ps = psum_in.tile([P, 2, GROUP_COLS], BF16, tag="in")
             for t in range(TILES_PER_GROUP):
                 cols = slice(t * P, (t + 1) * P)
                 nc.tensor.transpose(state_t_ps[:, 0, cols], kept["hyper_h_sb"][:, cols], ident_bf16[:])
                 nc.tensor.transpose(state_t_ps[:, 1, cols], kept["hyper_c_sb"][:, cols], ident_bf16[:])
-            state_t = four.tile([P, 2, GROUP_COLS], BF16)
-            nc.scalar.copy(out=state_t[:], in_=state_t_ps[:])
+            kept["state_t_ps"] = state_t_ps
+
+        def copy_inputs(group):
+            if outside(group):
+                return
+            kept = kept_tiles[group]
+            u_grouped = work.tile([P, GROUP_COLS * 4], BF16, align_bytes=64)
+            group_words(nc, kept["u_t_ps"], u_grouped[:])
+            state_t = work.tile([P, 2, GROUP_COLS], BF16, bufs=6)
+            nc.scalar.copy(out=state_t[:], in_=kept["state_t_ps"][:])
             kept["u_grouped"] = u_grouped
             kept["hyper_h_t"] = state_t[:, 0, :]
             kept["hyper_c_t"] = state_t[:, 1, :]
@@ -201,13 +247,13 @@ def tile_hyperlstmcell_pa_t_kernel(
             if outside(group):
                 return
             kept = kept_tiles[group]
-            u_codes = two.tile([P, GROUP_COLS], U32, align_bytes=64)
-            u_scales = two.tile([P, GROUP_COLS], U8, align_bytes=64)
+            u_codes = work.tile([P, GROUP_COLS], U32, align_bytes=64)
+            u_scales = work.tile([P, GROUP_COLS], U8, align_bytes=64)
             nc.vector.quantize_mx(out=u_codes[:].bitcast(FP8X4), scales=u_scales[:], in_=kept["u_grouped"][:])
             kept["u_codes"] = u_codes
             kept["u_scales"] = u_scales
 
-        def products(group, t):
+        def mx_product(group, t):
             if outside(group):
                 return
             kept = kept_tiles[group]
@@ -222,100 +268,115 @@ def tile_hyperlstmcell_pa_t_kernel(
                 start=True,
                 stop=True,
             )
+            kept["mx", t] = mx
+
+        def plain_product(group, t):
+            if outside(group):
+                return
+            kept = kept_tiles[group]
             plain = psum.tile([P, GATES, UNITS], F32, tag="plain")
             nc.tensor.matmul(
                 out=plain[:].rearrange("p g j -> p (g j)"),
-                lhsT=kept["hyper_h_t"][:, cols],
+                lhsT=kept["hyper_h_t"][:, t * P : (t + 1) * P],
                 rhs=whh_t[:],
                 start=True,
                 stop=True,
             )
-            kept["mx", t] = mx
             kept["plain", t] = plain
 
-        def add_and_sum(group, t):
+        def add_bias(group, t):
+            if outside(group):
+                return
+            kept = kept_tiles[group]
+            plain_bias = work.tile([P, GATES, UNITS], F32)
+            nc.vector.tensor_tensor(out=plain_bias[:], in0=kept["plain", t][:], in1=bias_all[:], op=ALU.add)
+            kept["plain_bias", t] = plain_bias
+
+        def add_products(group, t):
             if outside(group):
                 return
             kept = kept_tiles[group]
             if t == 0:
-                v = three.tile([P, TILES_PER_GROUP, GATES, UNITS], F32)
-                v_sum = three.tile([P, GROUP_STATS], F32)
-                sum_sq = three.tile([P, GROUP_STATS], F32)
-                squares = const.tile([P, TILES_PER_GROUP, GATES, UNITS], F32)
+                v = work.tile([P, TILES_PER_GROUP, GATES, UNITS], F32, bufs=3)
+                v_sum = work.tile([P, GROUP_STATS], F32, bufs=3)
                 kept["v"] = v
                 kept["v_sum"] = v_sum
-                kept["sum_sq"] = sum_sq
-                kept["squares"] = squares
-            mx, plain, v, v_sum = kept["mx", t], kept["plain", t], kept["v"], kept["v_sum"]
-            plain_bias = two.tile([P, GATES, UNITS], F32)
-            for step in range(GATES + LAG):
-                if step < GATES:
-                    nc.vector.tensor_tensor(
-                        out=plain_bias[:, step, :], in0=plain[:, step, :], in1=bias_all[:, step, :], op=ALU.add
-                    )
-                if step >= LAG:
-                    g = step - LAG
-                    nc.vector.scalar_tensor_tensor(
-                        out=v[:, t, g, :],
-                        in0=mx[:, g, :],
-                        scalar=1.0,
-                        in1=plain_bias[:, g, :],
-                        op0=ALU.mult,
-                        op1=ALU.add,
-                        accum_out=v_sum[:, t * GATES + g : t * GATES + g + 1],
-                    )
+            for g in range(GATES):
+                nc.vector.scalar_tensor_tensor(
+                    out=kept["v"][:, t, g, :],
+                    in0=kept["mx", t][:, g, :],
+                    scalar=1.0,
+                    in1=kept["plain_bias", t][:, g, :],
+                    op0=ALU.mult,
+                    op1=ALU.add,
+                    accum_out=kept["v_sum"][:, t * GATES + g : t * GATES + g + 1],
+                )
+
+        def new_moments(r):
+            if r < 0 or r >= N_GROUPS + CELL_LAG:
+                return
+            moments = work.tile([P, 2 * GROUP_STATS], F32)
+            shared_tiles[r]["moments"] = moments
+
+        def sum_squares(group, t):
+            if outside(group):
+                return
+            kept = kept_tiles[group]
             for g in range(GATES):
                 col = slice(t * GATES + g, t * GATES + g + 1)
                 nc.scalar.activation(
-                    out=kept["squares"][:, t, g, :],
-                    in_=v[:, t, g, :],
+                    out=squares[:, t, g, :],
+                    in_=kept["v"][:, t, g, :],
                     func=ACT.Square,
-                    bias=v_sum[:, col],
+                    bias=kept["v_sum"][:, col],
                     scale=-float(UNITS),
-                    accum_out=kept["sum_sq"][:, col],
+                    accum_out=shared_tiles[group]["moments"][:, col],
                 )
 
-        def gate_roots(group):
-            if outside(group):
+        def roots(r):
+            if r < 0 or r >= N_GROUPS + CELL_LAG:
                 return
-            kept = kept_tiles[group]
-            root = three.tile([P, GROUP_STATS], F32)
-            nc.gpsimd.tensor_tensor(out=root[:], in0=kept["sum_sq"][:], in1=half[:], op=ALU.pow)
-            kept["root"] = root
+            shared = shared_tiles[r]
+            cols = live_columns(r)
+            root = work.tile([P, ROUND_STATS], F32)
+            nc.gpsimd.tensor_tensor(out=root[:, cols], in0=shared["moments"][:, cols], in1=half[:, cols], op=ALU.pow)
+            shared["root"] = root
 
-        def gate_std(group):
-            if outside(group):
+        def std_eps(r):
+            if r < 0 or r >= N_GROUPS + CELL_LAG:
                 return
-            kept = kept_tiles[group]
-            std_eps = two.tile([P, GROUP_STATS], F32)
+            shared = shared_tiles[r]
+            cols = live_columns(r)
+            std = work.tile([P, ROUND_STATS], F32)
             nc.vector.tensor_scalar(
-                out=std_eps[:],
-                in0=kept["root"][:],
+                out=std[:, cols],
+                in0=shared["root"][:, cols],
                 scalar1=1.0 / (UNITS * (UNITS - 1) ** 0.5),
                 scalar2=EPS,
                 op0=ALU.mult,
                 op1=ALU.add,
             )
-            kept["std_eps"] = std_eps
+            shared["std"] = std
 
-        def gate_inv_std(group):
-            if outside(group):
+        def inv_std(r):
+            if r < 0 or r >= N_GROUPS + CELL_LAG:
                 return
-            kept = kept_tiles[group]
-            inv_std = two.tile([P, GROUP_STATS], F32)
-            nc.vector.reciprocal(out=inv_std[:], in_=kept["std_eps"][:])
-            kept["inv_std"] = inv_std
+            shared = shared_tiles[r]
+            cols = live_columns(r)
+            inv = work.tile([P, ROUND_STATS], F32)
+            nc.vector.reciprocal(out=inv[:, cols], in_=shared["std"][:, cols])
+            shared["inv"] = inv
 
         def gate_shift(group):
             if outside(group):
                 return
             kept = kept_tiles[group]
-            shift = two.tile([P, GROUP_STATS], F32)
+            shift = work.tile([P, GROUP_STATS], F32)
             nc.vector.scalar_tensor_tensor(
                 out=shift[:],
                 in0=kept["v_sum"][:],
                 scalar=-1.0 / UNITS,
-                in1=kept["inv_std"][:],
+                in1=shared_tiles[group]["inv"][:, 0:GROUP_STATS],
                 op0=ALU.mult,
                 op1=ALU.mult,
             )
@@ -325,15 +386,15 @@ def tile_hyperlstmcell_pa_t_kernel(
             if outside(group):
                 return
             kept = kept_tiles[group]
-            normed = two.tile([P, TILES_PER_GROUP, GATES, UNITS], F32)
-            for t in range(TILES_PER_GROUP):
-                for g in range(GATES):
+            normed = work.tile([P, TILES_PER_GROUP, GATES, UNITS], F32)
+            for g in range(GATES):
+                for t in range(TILES_PER_GROUP):
                     col = slice(t * GATES + g, t * GATES + g + 1)
                     nc.scalar.activation(
                         out=normed[:, t, g, :],
                         in_=kept["v"][:, t, g, :],
                         func=ACT.Identity,
-                        scale=kept["inv_std"][:, col],
+                        scale=shared_tiles[group]["inv"][:, col],
                         bias=kept["shift"][:, col],
                     )
             kept["normed"] = normed
@@ -345,8 +406,8 @@ def tile_hyperlstmcell_pa_t_kernel(
             norm_if = psum.tile([P, 2, TILES_PER_GROUP, P], F32, tag="norm_if")
             norm_go = psum.tile([P, 2, TILES_PER_GROUP, P], F32, tag="norm_go")
             banks = (norm_if, norm_go)
-            for t in range(TILES_PER_GROUP):
-                for g in range(GATES):
+            for g in range(GATES):
+                for t in range(TILES_PER_GROUP):
                     nc.tensor.transpose(banks[g // 2][:, g % 2, t, :], kept["normed"][:, t, g, :], ident_f32[:])
             kept["banks"] = banks
 
@@ -355,10 +416,10 @@ def tile_hyperlstmcell_pa_t_kernel(
                 return
             kept = kept_tiles[group]
             banks = kept["banks"]
-            gate_i = three.tile([P, GROUP_COLS], F32)
-            gate_f = three.tile([P, GROUP_COLS], F32)
-            gate_g = three.tile([P, GROUP_COLS], F32)
-            gate_o = three.tile([P, GROUP_COLS], F32)
+            gate_i = work.tile([P, GROUP_COLS], F32)
+            gate_f = work.tile([P, GROUP_COLS], F32)
+            gate_g = work.tile([P, GROUP_COLS], F32)
+            gate_o = work.tile([P, GROUP_COLS], F32)
             gates = (gate_i, gate_f, gate_g, gate_o)
             for g in range(GATES):
                 nc.scalar.activation(
@@ -370,17 +431,24 @@ def tile_hyperlstmcell_pa_t_kernel(
                 )
             kept["gates"] = gates
 
-        def cell_product(group):
+        def cell_parts(group):
             if outside(group):
                 return
             kept = kept_tiles[group]
             gate_i, gate_f, gate_g, gate_o = kept["gates"]
-            old_part = two.tile([P, GROUP_COLS], F32)
-            nc.vector.tensor_tensor(out=old_part[:], in0=gate_f[:], in1=kept["hyper_c_t"], op=ALU.mult)
-            new_part = two.tile([P, GROUP_COLS], F32)
-            nc.vector.tensor_tensor(out=new_part[:], in0=gate_i[:], in1=gate_g[:], op=ALU.mult)
-            raw_c = three.tile([P, GROUP_COLS], F32)
-            nc.vector.tensor_tensor(out=raw_c[:], in0=old_part[:], in1=new_part[:], op=ALU.add)
+            old_part = work.tile([P, GROUP_COLS], F32)
+            nc.gpsimd.tensor_tensor(out=old_part[:], in0=gate_f[:], in1=kept["hyper_c_t"], op=ALU.mult)
+            new_part = work.tile([P, GROUP_COLS], F32)
+            nc.gpsimd.tensor_tensor(out=new_part[:], in0=gate_i[:], in1=gate_g[:], op=ALU.mult)
+            kept["old_part"] = old_part
+            kept["new_part"] = new_part
+
+        def cell_sum(group):
+            if outside(group):
+                return
+            kept = kept_tiles[group]
+            raw_c = work.tile([P, GROUP_COLS], F32)
+            nc.vector.tensor_tensor(out=raw_c[:], in0=kept["old_part"][:], in1=kept["new_part"][:], op=ALU.add)
             kept["raw_c"] = raw_c
 
         def transpose_back(group):
@@ -392,87 +460,84 @@ def tile_hyperlstmcell_pa_t_kernel(
                 cols = slice(t * P, (t + 1) * P)
                 nc.tensor.transpose(back[:, 0, t, :], kept["raw_c"][:, cols], ident_f32[:])
                 nc.tensor.transpose(back[:, 1, t, :], kept["gates"][OUTPUT][:, cols], ident_f32[:])
-            gate_o_rows = three.tile([P, TILES_PER_GROUP, UNITS], F32)
-            nc.scalar.copy(out=gate_o_rows[:], in_=back[:, 1, :, :])
             kept["back"] = back
-            kept["gate_o_rows"] = gate_o_rows
 
-        def cell_stats(group):
+        def copy_output_gate(group):
             if outside(group):
                 return
             kept = kept_tiles[group]
-            raw_c_rows = kept["back"][:, 0, :, :]
-            c_stats = two.tile([P, TILES_PER_GROUP, 6], F32)
-            c_mean_var = three.tile([P, TILES_PER_GROUP, 2], F32)
+            gate_o_rows = work.tile([P, TILES_PER_GROUP, UNITS], F32, bufs=4)
+            nc.scalar.copy(out=gate_o_rows[:], in_=kept["back"][:, 1, :, :])
+            kept["gate_o_rows"] = gate_o_rows
+
+        def cell_moments(group):
+            if outside(group):
+                return
+            kept = kept_tiles[group]
+            c_stats = work.tile([P, TILES_PER_GROUP, 6], F32)
             for t in range(TILES_PER_GROUP):
-                nc.vector.bn_stats(out=c_stats[:, t, :], in_=raw_c_rows[:, t, :])
+                nc.vector.bn_stats(out=c_stats[:, t, :], in_=kept["back"][:, 0, t, :])
+            kept["c_stats"] = c_stats
+
+        def cell_centre(group):
+            if outside(group):
+                return
+            kept = kept_tiles[group]
+            c_mean_var = work.tile([P, TILES_PER_GROUP, 2], F32)
             for t in range(TILES_PER_GROUP):
-                nc.vector.bn_aggr(out=c_mean_var[:, t, :], in_=c_stats[:, t, :])
-            centred = two.tile([P, TILES_PER_GROUP, UNITS], F32)
+                nc.vector.bn_aggr(out=c_mean_var[:, t, :], in_=kept["c_stats"][:, t, :])
+            centred = work.tile([P, TILES_PER_GROUP, UNITS], F32, bufs=3)
             for t in range(TILES_PER_GROUP):
                 nc.vector.scalar_tensor_tensor(
                     out=centred[:, t, :],
-                    in0=raw_c_rows[:, t, :],
+                    in0=kept["back"][:, 0, t, :],
                     scalar=c_mean_var[:, t, 0:1],
-                    in1=gamma_c_all[:],
+                    in1=gamma_c_all,
                     op0=ALU.subtract,
                     op1=ALU.mult,
                 )
-            c_root = three.tile([P, TILES_PER_GROUP], F32)
-            nc.gpsimd.tensor_tensor(
-                out=c_root[:], in0=c_mean_var[:, :, 1], in1=half[:, 0:TILES_PER_GROUP], op=ALU.pow
-            )
+            kept["c_mean_var"] = c_mean_var
             kept["centred"] = centred
-            kept["c_root"] = c_root
 
-        def cell_std(group):
+        def cell_variance(group):
             if outside(group):
                 return
-            kept = kept_tiles[group]
-            c_std_eps = two.tile([P, TILES_PER_GROUP], F32)
-            nc.vector.tensor_scalar(
-                out=c_std_eps[:],
-                in0=kept["c_root"][:],
-                scalar1=(UNITS / (UNITS - 1)) ** 0.5,
-                scalar2=EPS,
-                op0=ALU.mult,
-                op1=ALU.add,
+            nc.vector.tensor_scalar_mul(
+                out=shared_tiles[group + CELL_LAG]["moments"][:, GROUP_STATS:ROUND_STATS],
+                in0=kept_tiles[group]["c_mean_var"][:, :, 1],
+                scalar1=float(UNITS**3),
             )
-            kept["c_std_eps"] = c_std_eps
-
-        def cell_inv_std(group):
-            if outside(group):
-                return
-            kept = kept_tiles[group]
-            c_inv_std = two.tile([P, TILES_PER_GROUP], F32)
-            nc.vector.reciprocal(out=c_inv_std[:], in_=kept["c_std_eps"][:])
-            kept["c_inv_std"] = c_inv_std
 
         def cell_out(group):
             if outside(group):
                 return
             kept = kept_tiles[group]
-            new_c = three.tile([P, TILES_PER_GROUP, UNITS], F32)
+            new_c = work.tile([P, TILES_PER_GROUP, UNITS], F32, bufs=3)
             for t in range(TILES_PER_GROUP):
                 nc.vector.scalar_tensor_tensor(
                     out=new_c[:, t, :],
                     in0=kept["centred"][:, t, :],
-                    scalar=kept["c_inv_std"][:, t : t + 1],
-                    in1=beta_c_all[:],
+                    scalar=shared_tiles[group + CELL_LAG]["inv"][:, GROUP_STATS + t : GROUP_STATS + t + 1],
+                    in1=beta_c_all,
                     op0=ALU.mult,
                     op1=ALU.add,
                 )
-            new_c_flat = new_c[:].rearrange("p t j -> p (t j)")
-            nc.sync.dma_start(out=new_c_rows[:, group * GROUP_COLS : (group + 1) * GROUP_COLS], in_=new_c_flat)
-            tanh_c = two.tile([P, GROUP_COLS], F32)
-            nc.scalar.activation(out=tanh_c[:], in_=new_c_flat, func=ACT.Tanh)
+            kept["new_c"] = new_c[:].rearrange("p t j -> p (t j)")
+            nc.sync.dma_start(out=new_c_rows[:, group * GROUP_COLS : (group + 1) * GROUP_COLS], in_=kept["new_c"])
+
+        def cell_tanh(group):
+            if outside(group):
+                return
+            kept = kept_tiles[group]
+            tanh_c = work.tile([P, GROUP_COLS], F32)
+            nc.scalar.activation(out=tanh_c[:], in_=kept["new_c"], func=ACT.Tanh)
             kept["tanh_c"] = tanh_c
 
         def hidden_out(group):
             if outside(group):
                 return
             kept = kept_tiles[group]
-            new_h = three.tile([P, GROUP_COLS], F32)
+            new_h = work.tile([P, GROUP_COLS], F32, bufs=3)
             nc.vector.tensor_tensor(
                 out=new_h[:],
                 in0=kept["gate_o_rows"][:].rearrange("p t j -> p (t j)"),
@@ -482,25 +547,36 @@ def tile_hyperlstmcell_pa_t_kernel(
             nc.sync.dma_start(out=new_h_rows[:, group * GROUP_COLS : (group + 1) * GROUP_COLS], in_=new_h[:])
 
         with tc.manual_schedule():
-            for i in range(-2, N_GROUPS + 5):
-                load(i + 4)
-                products(i, 1)
-                transpose_back(i - 3)
-                add_and_sum(i, 0)
-                add_and_sum(i, 1)
-                gate_roots(i)
-                gate_std(i - 1)
-                cell_std(i - 4)
-                hidden_out(i - 5)
-                gate_inv_std(i - 1)
-                cell_inv_std(i - 4)
-                quantise(i + 1)
+            for i in range(-3, N_GROUPS + 5):
+                load(i + 5)
+                new_moments(i)
+                activate(i - 2)
+                add_bias(i, 0)
+                plain_product(i, 1)
+                cell_parts(i - 2)
+                cell_moments(i - 3)
+                copy_output_gate(i - 3)
+                cell_tanh(i - 5)
+                add_products(i, 0)
+                transpose_inputs(i + 3)
+                sum_squares(i, 0)
+                mx_product(i + 1, 0)
+                add_bias(i, 1)
+                plain_product(i + 1, 0)
+                cell_centre(i - 3)
+                copy_inputs(i + 3)
+                add_products(i, 1)
+                mx_product(i + 1, 1)
+                sum_squares(i, 1)
+                cell_variance(i - 3)
+                roots(i)
+                std_eps(i - 1)
+                quantise(i + 2)
+                inv_std(i - 1)
+                cell_sum(i - 2)
+                transpose_back(i - 2)
                 gate_shift(i - 1)
-                cell_product(i - 2)
                 normalise(i - 1)
-                transpose_inputs(i + 2)
-                products(i + 1, 0)
                 transpose_normed(i - 1)
                 cell_out(i - 4)
-                activate(i - 1)
-                cell_stats(i - 3)
+                hidden_out(i - 5)

@@ -33,6 +33,8 @@ OUTPUT = 3
 CELL_LAG = 3
 ROUND_STATS = GROUP_STATS + TILES_PER_GROUP
 
+SCALAR_GATES = 2
+
 LOADS_AHEAD = 4
 
 FLOPS = 2 * BATCH * K * GATES * UNITS + 2 * BATCH * UNITS * GATES * UNITS
@@ -151,7 +153,7 @@ def tile_hyperlstmcell_pa_t_kernel(
             out=whh_rows[:].rearrange("p (g k) -> p g k", g=GATES),
             in_=hc_Whh.rearrange("(g p) k -> p g k", p=P),
         )
-        whh_t_ps = psum_in.tile([P, GATES * P], BF16, tag="in")
+        whh_t_ps = psum.tile([P, GATES * P], BF16, tag="norm_if")
         for g in range(GATES):
             nc.tensor.transpose(
                 whh_t_ps[:, g * P : (g + 1) * P], whh_rows[:, g * UNITS : (g + 1) * UNITS], ident_bf16[:]
@@ -170,7 +172,7 @@ def tile_hyperlstmcell_pa_t_kernel(
         )
         ones = const.tile([P, P], BF16)
         nc.vector.memset(ones[:], 1.0)
-        bias_ps = psum_in.tile([P, GATES, UNITS], F32, tag="in")
+        bias_ps = psum.tile([P, GATES, UNITS], F32, tag="norm_go")
         nc.tensor.matmul(
             out=bias_ps[:].rearrange("p g j -> p (g j)"),
             lhsT=ones[:],
@@ -180,7 +182,7 @@ def tile_hyperlstmcell_pa_t_kernel(
         )
         bias_all = const.tile([P, GATES, UNITS], BF16)
         nc.vector.tensor_copy(out=bias_all[:], in_=bias_ps[:])
-        cell_ps = psum_in.tile([P, 2, UNITS], F32, tag="in")
+        cell_ps = psum.tile([P, 2, UNITS], F32, tag="back")
         nc.tensor.matmul(
             out=cell_ps[:].rearrange("p c j -> p (c j)"),
             lhsT=ones[:],
@@ -197,7 +199,7 @@ def tile_hyperlstmcell_pa_t_kernel(
         nc.vector.memset(gate_rows[:], 0.0)
         nc.scalar.dma_start(out=gate_rows[0:GATES, :], in_=hc_ln_gamma)
         nc.scalar.dma_start(out=gate_rows[GATES : 2 * GATES, :], in_=hc_ln_beta)
-        gate_cols_ps = psum_in.tile([P, P], BF16, tag="in")
+        gate_cols_ps = psum.tile([P, P], BF16, tag="back")
         nc.tensor.transpose(gate_cols_ps[:], gate_rows[:], ident_bf16[:])
         gate_cols = const.tile([P, 2 * GATES], F32)
         nc.vector.tensor_copy(out=gate_cols[:], in_=gate_cols_ps[:, 0 : 2 * GATES])
@@ -237,7 +239,7 @@ def tile_hyperlstmcell_pa_t_kernel(
             kept = kept_tiles[group]
             u_grouped = work.tile([P, GROUP_COLS * 4], BF16, align_bytes=64)
             group_words(nc, kept["u_t_ps"], u_grouped[:])
-            state_t = work.tile([P, 2, GROUP_COLS], BF16, bufs=6)
+            state_t = work.tile([P, 2, GROUP_COLS], BF16, bufs=5)
             nc.scalar.copy(out=state_t[:], in_=kept["state_t_ps"][:])
             kept["u_grouped"] = u_grouped
             kept["hyper_h_t"] = state_t[:, 0, :]
@@ -382,12 +384,12 @@ def tile_hyperlstmcell_pa_t_kernel(
             )
             kept["shift"] = shift
 
-        def normalise(group):
+        def normalise_on_scalar(group):
             if outside(group):
                 return
             kept = kept_tiles[group]
             normed = work.tile([P, TILES_PER_GROUP, GATES, UNITS], F32)
-            for g in range(GATES):
+            for g in range(SCALAR_GATES):
                 for t in range(TILES_PER_GROUP):
                     col = slice(t * GATES + g, t * GATES + g + 1)
                     nc.scalar.activation(
@@ -398,6 +400,22 @@ def tile_hyperlstmcell_pa_t_kernel(
                         bias=kept["shift"][:, col],
                     )
             kept["normed"] = normed
+
+        def normalise_on_vector(group):
+            if outside(group):
+                return
+            kept = kept_tiles[group]
+            for g in range(SCALAR_GATES, GATES):
+                for t in range(TILES_PER_GROUP):
+                    col = slice(t * GATES + g, t * GATES + g + 1)
+                    nc.vector.tensor_scalar(
+                        out=kept["normed"][:, t, g, :],
+                        in0=kept["v"][:, t, g, :],
+                        scalar1=shared_tiles[group]["inv"][:, col],
+                        scalar2=kept["shift"][:, col],
+                        op0=ALU.mult,
+                        op1=ALU.add,
+                    )
 
         def transpose_normed(group):
             if outside(group):
@@ -419,7 +437,7 @@ def tile_hyperlstmcell_pa_t_kernel(
             gate_i = work.tile([P, GROUP_COLS], F32)
             gate_f = work.tile([P, GROUP_COLS], F32)
             gate_g = work.tile([P, GROUP_COLS], F32)
-            gate_o = work.tile([P, GROUP_COLS], F32)
+            gate_o = work.tile([P, GROUP_COLS], F32, bufs=5)
             gates = (gate_i, gate_f, gate_g, gate_o)
             for g in range(GATES):
                 nc.scalar.activation(
@@ -451,24 +469,20 @@ def tile_hyperlstmcell_pa_t_kernel(
             nc.vector.tensor_tensor(out=raw_c[:], in0=kept["old_part"][:], in1=kept["new_part"][:], op=ALU.add)
             kept["raw_c"] = raw_c
 
-        def transpose_back(group):
-            if outside(group):
+        def transpose_back(cell_group, gate_group):
+            if outside(cell_group) and outside(gate_group):
                 return
-            kept = kept_tiles[group]
             back = psum.tile([P, 2, TILES_PER_GROUP, UNITS], F32, tag="back")
             for t in range(TILES_PER_GROUP):
                 cols = slice(t * P, (t + 1) * P)
-                nc.tensor.transpose(back[:, 0, t, :], kept["raw_c"][:, cols], ident_f32[:])
-                nc.tensor.transpose(back[:, 1, t, :], kept["gates"][OUTPUT][:, cols], ident_f32[:])
-            kept["back"] = back
-
-        def copy_output_gate(group):
-            if outside(group):
-                return
-            kept = kept_tiles[group]
-            gate_o_rows = work.tile([P, TILES_PER_GROUP, UNITS], F32, bufs=4)
-            nc.scalar.copy(out=gate_o_rows[:], in_=kept["back"][:, 1, :, :])
-            kept["gate_o_rows"] = gate_o_rows
+                if not outside(cell_group):
+                    nc.tensor.transpose(back[:, 0, t, :], kept_tiles[cell_group]["raw_c"][:, cols], ident_f32[:])
+                if not outside(gate_group):
+                    nc.tensor.transpose(back[:, 1, t, :], kept_tiles[gate_group]["gates"][OUTPUT][:, cols], ident_f32[:])
+            if not outside(cell_group):
+                kept_tiles[cell_group]["raw_c_rows"] = back[:, 0, :, :]
+            if not outside(gate_group):
+                kept_tiles[gate_group]["gate_o_rows"] = back[:, 1, :, :]
 
         def cell_moments(group):
             if outside(group):
@@ -476,7 +490,7 @@ def tile_hyperlstmcell_pa_t_kernel(
             kept = kept_tiles[group]
             c_stats = work.tile([P, TILES_PER_GROUP, 6], F32)
             for t in range(TILES_PER_GROUP):
-                nc.vector.bn_stats(out=c_stats[:, t, :], in_=kept["back"][:, 0, t, :])
+                nc.vector.bn_stats(out=c_stats[:, t, :], in_=kept["raw_c_rows"][:, t, :])
             kept["c_stats"] = c_stats
 
         def cell_centre(group):
@@ -490,7 +504,7 @@ def tile_hyperlstmcell_pa_t_kernel(
             for t in range(TILES_PER_GROUP):
                 nc.vector.scalar_tensor_tensor(
                     out=centred[:, t, :],
-                    in0=kept["back"][:, 0, t, :],
+                    in0=kept["raw_c_rows"][:, t, :],
                     scalar=c_mean_var[:, t, 0:1],
                     in1=gamma_c_all,
                     op0=ALU.subtract,
@@ -540,31 +554,31 @@ def tile_hyperlstmcell_pa_t_kernel(
             new_h = work.tile([P, GROUP_COLS], F32, bufs=3)
             nc.vector.tensor_tensor(
                 out=new_h[:],
-                in0=kept["gate_o_rows"][:].rearrange("p t j -> p (t j)"),
+                in0=kept["gate_o_rows"].rearrange("p t j -> p (t j)"),
                 in1=kept["tanh_c"][:],
                 op=ALU.mult,
             )
             nc.sync.dma_start(out=new_h_rows[:, group * GROUP_COLS : (group + 1) * GROUP_COLS], in_=new_h[:])
 
         with tc.manual_schedule():
-            for i in range(-3, N_GROUPS + 5):
-                load(i + 5)
+            for i in range(-2, N_GROUPS + 6):
+                load(i + 4)
                 new_moments(i)
                 activate(i - 2)
                 add_bias(i, 0)
                 plain_product(i, 1)
                 cell_parts(i - 2)
                 cell_moments(i - 3)
-                copy_output_gate(i - 3)
+                hidden_out(i - 6)
                 cell_tanh(i - 5)
+                transpose_inputs(i + 2)
                 add_products(i, 0)
-                transpose_inputs(i + 3)
-                sum_squares(i, 0)
+                copy_inputs(i + 2)
                 mx_product(i + 1, 0)
                 add_bias(i, 1)
                 plain_product(i + 1, 0)
                 cell_centre(i - 3)
-                copy_inputs(i + 3)
+                sum_squares(i, 0)
                 add_products(i, 1)
                 mx_product(i + 1, 1)
                 sum_squares(i, 1)
@@ -574,9 +588,9 @@ def tile_hyperlstmcell_pa_t_kernel(
                 quantise(i + 2)
                 inv_std(i - 1)
                 cell_sum(i - 2)
-                transpose_back(i - 2)
+                transpose_back(i - 2, i - 5)
                 gate_shift(i - 1)
-                normalise(i - 1)
-                transpose_normed(i - 1)
+                normalise_on_scalar(i - 1)
                 cell_out(i - 4)
-                hidden_out(i - 5)
+                normalise_on_vector(i - 1)
+                transpose_normed(i - 1)

@@ -33,7 +33,7 @@ OUTPUT = 3
 CELL_LAG = 3
 ROUND_STATS = GROUP_STATS + TILES_PER_GROUP
 
-SCALAR_GATES = 2
+SCALAR_GATES = 1
 
 LOADS_AHEAD = 4
 

from contextlib import ExitStack

import concourse.mybir as mybir
from concourse.masks import make_identity

F32 = mybir.dt.float32
BF16 = mybir.dt.bfloat16
U32 = mybir.dt.uint32
U8 = mybir.dt.uint8
FP8X4 = mybir.dt.float8_e4m3fn_x4
ALU = mybir.AluOpType
ACT = mybir.ActivationFunctionType

P = 128
BATCH = 4096
IN = 256
K = 2 * IN
UNITS = 128
GATES = 4
EPS = 1e-6

N_TILES = BATCH // P
TILES_PER_GROUP = 2
N_GROUPS = N_TILES // TILES_PER_GROUP
GROUP_COLS = TILES_PER_GROUP * P
GROUP_STATS = TILES_PER_GROUP * GATES
WORDS = IN // 2

GATE_FUNCS = (ACT.Sigmoid, ACT.Sigmoid, ACT.Tanh, ACT.Sigmoid)
FORGET = 1
OUTPUT = 3

CELL_LAG = 3
ROUND_STATS = GROUP_STATS + TILES_PER_GROUP

SCALAR_GATES = 1

LOADS_AHEAD = 4

FLOPS = 2 * BATCH * K * GATES * UNITS + 2 * BATCH * UNITS * GATES * UNITS


def transpose_words(nc, psum, ident_f32, halves):
    k_first = psum.tile([P, 2, 2, P], F32, tag="in")
    for i in range(2):
        for u in range(2):
            nc.tensor.transpose(k_first[:, i, u, :], halves[i][u], ident_f32)
    return k_first


def group_words(nc, k_first, grouped):
    nc.scalar.copy(
        out=grouped.bitcast(F32).rearrange("p (i r u) -> p i r u", i=2, u=2),
        in_=k_first[:].rearrange("p i u r -> p i r u"),
    )


def tile_hyperlstmcell_pa_t_kernel(
    tc,
    x,
    h,
    hyper_h,
    hyper_c,
    hc_Wih,
    hc_bih,
    hc_Whh,
    hc_ln_gamma,
    hc_ln_beta,
    hc_lnc_gamma,
    hc_lnc_beta,
    out_0,
    out_1,
):
    nc = tc.nc
    with ExitStack() as ctx:
        const = ctx.enter_context(tc.tile_pool(name="const", bufs=1))
        work = ctx.enter_context(tc.tile_pool(name="work", bufs=2))
        psum_in = ctx.enter_context(tc.psum_pool(name="psum_in", bufs=2))
        psum_mx = ctx.enter_context(tc.psum_pool(name="psum_mx", bufs=2))
        psum = ctx.enter_context(tc.psum_pool(name="psum", bufs=1))

        x_rows = x.rearrange("(p r) k -> p (r k)", r=N_TILES)
        h_rows = h.rearrange("(p r) k -> p (r k)", r=N_TILES)
        hyper_h_rows = hyper_h.rearrange("(p r) k -> p (r k)", r=N_TILES)
        hyper_c_rows = hyper_c.rearrange("(p r) k -> p (r k)", r=N_TILES)
        new_h_rows = out_0.rearrange("(p r) k -> p (r k)", r=N_TILES)
        new_c_rows = out_1.rearrange("(p r) k -> p (r k)", r=N_TILES)

        kept_tiles = [dict() for group in range(N_GROUPS)]
        shared_tiles = [dict() for r in range(N_GROUPS + CELL_LAG)]

        def outside(group):
            return group < 0 or group >= N_GROUPS

        def live_columns(r):
            first = 0 if r < N_GROUPS else GROUP_STATS
            last = ROUND_STATS if r >= CELL_LAG else GROUP_STATS
            return slice(first, last)

        def load(group):
            if outside(group):
                return
            x_sb = work.tile([P, TILES_PER_GROUP * IN], BF16, bufs=LOADS_AHEAD)
            h_sb = work.tile([P, TILES_PER_GROUP * IN], BF16, bufs=LOADS_AHEAD)
            hyper_h_sb = work.tile([P, GROUP_COLS], BF16, bufs=LOADS_AHEAD)
            hyper_c_sb = work.tile([P, GROUP_COLS], BF16, bufs=LOADS_AHEAD)
            wide = slice(group * TILES_PER_GROUP * IN, (group + 1) * TILES_PER_GROUP * IN)
            narrow = slice(group * GROUP_COLS, (group + 1) * GROUP_COLS)
            nc.sync.dma_start(out=x_sb[:], in_=x_rows[:, wide])
            nc.sync.dma_start(out=h_sb[:], in_=h_rows[:, wide])
            nc.sync.dma_start(out=hyper_h_sb[:], in_=hyper_h_rows[:, narrow])
            nc.sync.dma_start(out=hyper_c_sb[:], in_=hyper_c_rows[:, narrow])
            kept_tiles[group]["x_sb"] = x_sb
            kept_tiles[group]["h_sb"] = h_sb
            kept_tiles[group]["hyper_h_sb"] = hyper_h_sb
            kept_tiles[group]["hyper_c_sb"] = hyper_c_sb

        wih_rows = const.tile([P, GATES * K], BF16)
        nc.sync.dma_start(
            out=wih_rows[:].rearrange("p (g k) -> p g k", g=GATES),
            in_=hc_Wih.rearrange("(g p) k -> p g k", p=P),
        )
        load(0)
        load(1)

        ident_f32 = const.tile([P, P], F32)
        make_identity(nc, ident_f32[:])
        ident_bf16 = const.tile([P, P], BF16)
        make_identity(nc, ident_bf16[:])

        wih_words = wih_rows[:].bitcast(F32)
        wih_grouped = const.tile([P, GATES * P * 4], BF16, align_bytes=64)
        wih_codes = const.tile([P, GATES * P], U32, align_bytes=64)
        wih_scales = const.tile([P, GATES * P], U8, align_bytes=64)
        for pair in range(GATES // 2):
            wih_t_ps = transpose_words(
                nc,
                psum_in,
                ident_f32[:],
                [
                    (
                        wih_words[:, 2 * g * WORDS : (2 * g + 1) * WORDS],
                        wih_words[:, (2 * g + 1) * WORDS : (2 * g + 2) * WORDS],
                    )
                    for g in (2 * pair, 2 * pair + 1)
                ],
            )
            group_words(nc, wih_t_ps, wih_grouped[:, 2 * pair * P * 4 : (2 * pair + 2) * P * 4])
        nc.vector.quantize_mx(out=wih_codes[:].bitcast(FP8X4), scales=wih_scales[:], in_=wih_grouped[:])

        whh_rows = const.tile([P, GATES * UNITS], BF16)
        nc.scalar.dma_start(
            out=whh_rows[:].rearrange("p (g k) -> p g k", g=GATES),
            in_=hc_Whh.rearrange("(g p) k -> p g k", p=P),
        )
        whh_t_ps = psum.tile([P, GATES * P], BF16, tag="norm_if")
        for g in range(GATES):
            nc.tensor.transpose(
                whh_t_ps[:, g * P : (g + 1) * P], whh_rows[:, g * UNITS : (g + 1) * UNITS], ident_bf16[:]
            )
        whh_t = const.tile([P, GATES * P], BF16)
        nc.vector.tensor_copy(out=whh_t[:], in_=whh_t_ps[:])

        vector_rows = const.tile([P, (GATES + 2) * UNITS], BF16)
        nc.vector.memset(vector_rows[:], 0.0)
        nc.scalar.dma_start(out=vector_rows[0:1, 0 : GATES * UNITS], in_=hc_bih.rearrange("(o n) -> o n", o=1))
        nc.scalar.dma_start(
            out=vector_rows[0:1, GATES * UNITS : (GATES + 1) * UNITS], in_=hc_lnc_gamma.rearrange("(o n) -> o n", o=1)
        )
        nc.scalar.dma_start(
            out=vector_rows[0:1, (GATES + 1) * UNITS : (GATES + 2) * UNITS], in_=hc_lnc_beta.rearrange("(o n) -> o n", o=1)
        )
        ones = const.tile([P, P], BF16)
        nc.vector.memset(ones[:], 1.0)
        bias_ps = psum.tile([P, GATES, UNITS], F32, tag="norm_go")
        nc.tensor.matmul(
            out=bias_ps[:].rearrange("p g j -> p (g j)"),
            lhsT=ones[:],
            rhs=vector_rows[:, 0 : GATES * UNITS],
            start=True,
            stop=True,
        )
        bias_all = const.tile([P, GATES, UNITS], BF16)
        nc.vector.tensor_copy(out=bias_all[:], in_=bias_ps[:])
        cell_ps = psum.tile([P, 2, UNITS], F32, tag="back")
        nc.tensor.matmul(
            out=cell_ps[:].rearrange("p c j -> p (c j)"),
            lhsT=ones[:],
            rhs=vector_rows[:, GATES * UNITS : (GATES + 2) * UNITS],
            start=True,
            stop=True,
        )
        cell_all = const.tile([P, 2, UNITS], BF16)
        nc.vector.tensor_copy(out=cell_all[:], in_=cell_ps[:])
        gamma_c_all = cell_all[:, 0, :]
        beta_c_all = cell_all[:, 1, :]

        gate_rows = const.tile([P, P], BF16)
        nc.vector.memset(gate_rows[:], 0.0)
        nc.scalar.dma_start(out=gate_rows[0:GATES, :], in_=hc_ln_gamma)
        nc.scalar.dma_start(out=gate_rows[GATES : 2 * GATES, :], in_=hc_ln_beta)
        gate_cols_ps = psum.tile([P, P], BF16, tag="back")
        nc.tensor.transpose(gate_cols_ps[:], gate_rows[:], ident_bf16[:])
        gate_cols = const.tile([P, 2 * GATES], F32)
        nc.vector.tensor_copy(out=gate_cols[:], in_=gate_cols_ps[:, 0 : 2 * GATES])
        forget_beta = gate_cols[:, GATES + FORGET : GATES + FORGET + 1]
        nc.vector.tensor_scalar_add(out=forget_beta, in0=forget_beta, scalar1=1.0)

        half = const.tile([P, ROUND_STATS], F32)
        nc.vector.memset(half[:], 0.5)

        squares = const.tile([P, TILES_PER_GROUP, GATES, UNITS], F32)

        def transpose_inputs(group):
            if outside(group):
                return
            kept = kept_tiles[group]
            x_words = kept["x_sb"][:].bitcast(F32)
            h_words = kept["h_sb"][:].bitcast(F32)
            kept["u_t_ps"] = transpose_words(
                nc,
                psum_in,
                ident_f32[:],
                [
                    (x_words[:, t * WORDS : (t + 1) * WORDS], h_words[:, t * WORDS : (t + 1) * WORDS])
                    for t in range(TILES_PER_GROUP)
                ],
            )
            state_t_ps = psum_in.tile([P, 2, GROUP_COLS], BF16, tag="in")
            for t in range(TILES_PER_GROUP):
                cols = slice(t * P, (t + 1) * P)
                nc.tensor.transpose(state_t_ps[:, 0, cols], kept["hyper_h_sb"][:, cols], ident_bf16[:])
                nc.tensor.transpose(state_t_ps[:, 1, cols], kept["hyper_c_sb"][:, cols], ident_bf16[:])
            kept["state_t_ps"] = state_t_ps

        def copy_inputs(group):
            if outside(group):
                return
            kept = kept_tiles[group]
            u_grouped = work.tile([P, GROUP_COLS * 4], BF16, align_bytes=64)
            group_words(nc, kept["u_t_ps"], u_grouped[:])
            state_t = work.tile([P, 2, GROUP_COLS], BF16, bufs=5)
            nc.scalar.copy(out=state_t[:], in_=kept["state_t_ps"][:])
            kept["u_grouped"] = u_grouped
            kept["hyper_h_t"] = state_t[:, 0, :]
            kept["hyper_c_t"] = state_t[:, 1, :]

        def quantise(group):
            if outside(group):
                return
            kept = kept_tiles[group]
            u_codes = work.tile([P, GROUP_COLS], U32, align_bytes=64)
            u_scales = work.tile([P, GROUP_COLS], U8, align_bytes=64)
            nc.vector.quantize_mx(out=u_codes[:].bitcast(FP8X4), scales=u_scales[:], in_=kept["u_grouped"][:])
            kept["u_codes"] = u_codes
            kept["u_scales"] = u_scales

        def mx_product(group, t):
            if outside(group):
                return
            kept = kept_tiles[group]
            cols = slice(t * P, (t + 1) * P)
            mx = psum_mx.tile([P, GATES, UNITS], F32)
            nc.tensor.matmul_mx(
                out=mx[:].rearrange("p g j -> p (g j)"),
                lhsT=kept["u_codes"][:, cols].bitcast(FP8X4),
                lhsT_scale=kept["u_scales"][:, cols],
                rhs=wih_codes[:].bitcast(FP8X4),
                rhs_scale=wih_scales[:],
                start=True,
                stop=True,
            )
            kept["mx", t] = mx

        def plain_product(group, t):
            if outside(group):
                return
            kept = kept_tiles[group]
            plain = psum.tile([P, GATES, UNITS], F32, tag="plain")
            nc.tensor.matmul(
                out=plain[:].rearrange("p g j -> p (g j)"),
                lhsT=kept["hyper_h_t"][:, t * P : (t + 1) * P],
                rhs=whh_t[:],
                start=True,
                stop=True,
            )
            kept["plain", t] = plain

        def add_bias(group, t):
            if outside(group):
                return
            kept = kept_tiles[group]
            plain_bias = work.tile([P, GATES, UNITS], F32)
            nc.vector.tensor_tensor(out=plain_bias[:], in0=kept["plain", t][:], in1=bias_all[:], op=ALU.add)
            kept["plain_bias", t] = plain_bias

        def add_products(group, t):
            if outside(group):
                return
            kept = kept_tiles[group]
            if t == 0:
                v = work.tile([P, TILES_PER_GROUP, GATES, UNITS], F32, bufs=3)
                v_sum = work.tile([P, GROUP_STATS], F32, bufs=3)
                kept["v"] = v
                kept["v_sum"] = v_sum
            for g in range(GATES):
                nc.vector.scalar_tensor_tensor(
                    out=kept["v"][:, t, g, :],
                    in0=kept["mx", t][:, g, :],
                    scalar=1.0,
                    in1=kept["plain_bias", t][:, g, :],
                    op0=ALU.mult,
                    op1=ALU.add,
                    accum_out=kept["v_sum"][:, t * GATES + g : t * GATES + g + 1],
                )

        def new_moments(r):
            if r < 0 or r >= N_GROUPS + CELL_LAG:
                return
            moments = work.tile([P, 2 * GROUP_STATS], F32)
            shared_tiles[r]["moments"] = moments

        def sum_squares(group, t):
            if outside(group):
                return
            kept = kept_tiles[group]
            for g in range(GATES):
                col = slice(t * GATES + g, t * GATES + g + 1)
                nc.scalar.activation(
                    out=squares[:, t, g, :],
                    in_=kept["v"][:, t, g, :],
                    func=ACT.Square,
                    bias=kept["v_sum"][:, col],
                    scale=-float(UNITS),
                    accum_out=shared_tiles[group]["moments"][:, col],
                )

        def roots(r):
            if r < 0 or r >= N_GROUPS + CELL_LAG:
                return
            shared = shared_tiles[r]
            cols = live_columns(r)
            root = work.tile([P, ROUND_STATS], F32)
            nc.gpsimd.tensor_tensor(out=root[:, cols], in0=shared["moments"][:, cols], in1=half[:, cols], op=ALU.pow)
            shared["root"] = root

        def std_eps(r):
            if r < 0 or r >= N_GROUPS + CELL_LAG:
                return
            shared = shared_tiles[r]
            cols = live_columns(r)
            std = work.tile([P, ROUND_STATS], F32)
            nc.vector.tensor_scalar(
                out=std[:, cols],
                in0=shared["root"][:, cols],
                scalar1=1.0 / (UNITS * (UNITS - 1) ** 0.5),
                scalar2=EPS,
                op0=ALU.mult,
                op1=ALU.add,
            )
            shared["std"] = std

        def inv_std(r):
            if r < 0 or r >= N_GROUPS + CELL_LAG:
                return
            shared = shared_tiles[r]
            cols = live_columns(r)
            inv = work.tile([P, ROUND_STATS], F32)
            nc.vector.reciprocal(out=inv[:, cols], in_=shared["std"][:, cols])
            shared["inv"] = inv

        def gate_shift(group):
            if outside(group):
                return
            kept = kept_tiles[group]
            shift = work.tile([P, GROUP_STATS], F32)
            nc.vector.scalar_tensor_tensor(
                out=shift[:],
                in0=kept["v_sum"][:],
                scalar=-1.0 / UNITS,
                in1=shared_tiles[group]["inv"][:, 0:GROUP_STATS],
                op0=ALU.mult,
                op1=ALU.mult,
            )
            kept["shift"] = shift

        def normalise_on_scalar(group):
            if outside(group):
                return
            kept = kept_tiles[group]
            normed = work.tile([P, TILES_PER_GROUP, GATES, UNITS], F32)
            for g in range(SCALAR_GATES):
                for t in range(TILES_PER_GROUP):
                    col = slice(t * GATES + g, t * GATES + g + 1)
                    nc.scalar.activation(
                        out=normed[:, t, g, :],
                        in_=kept["v"][:, t, g, :],
                        func=ACT.Identity,
                        scale=shared_tiles[group]["inv"][:, col],
                        bias=kept["shift"][:, col],
                    )
            kept["normed"] = normed

        def normalise_on_vector(group):
            if outside(group):
                return
            kept = kept_tiles[group]
            for g in range(SCALAR_GATES, GATES):
                for t in range(TILES_PER_GROUP):
                    col = slice(t * GATES + g, t * GATES + g + 1)
                    nc.vector.tensor_scalar(
                        out=kept["normed"][:, t, g, :],
                        in0=kept["v"][:, t, g, :],
                        scalar1=shared_tiles[group]["inv"][:, col],
                        scalar2=kept["shift"][:, col],
                        op0=ALU.mult,
                        op1=ALU.add,
                    )

        def transpose_normed(group):
            if outside(group):
                return
            kept = kept_tiles[group]
            norm_if = psum.tile([P, 2, TILES_PER_GROUP, P], F32, tag="norm_if")
            norm_go = psum.tile([P, 2, TILES_PER_GROUP, P], F32, tag="norm_go")
            banks = (norm_if, norm_go)
            for g in range(GATES):
                for t in range(TILES_PER_GROUP):
                    nc.tensor.transpose(banks[g // 2][:, g % 2, t, :], kept["normed"][:, t, g, :], ident_f32[:])
            kept["banks"] = banks

        def activate(group):
            if outside(group):
                return
            kept = kept_tiles[group]
            banks = kept["banks"]
            gate_i = work.tile([P, GROUP_COLS], F32)
            gate_f = work.tile([P, GROUP_COLS], F32)
            gate_g = work.tile([P, GROUP_COLS], F32)
            gate_o = work.tile([P, GROUP_COLS], F32, bufs=5)
            gates = (gate_i, gate_f, gate_g, gate_o)
            for g in range(GATES):
                nc.scalar.activation(
                    out=gates[g][:],
                    in_=banks[g // 2][:, g % 2, :, :].rearrange("p t b -> p (t b)"),
                    func=GATE_FUNCS[g],
                    scale=gate_cols[:, g : g + 1],
                    bias=gate_cols[:, GATES + g : GATES + g + 1],
                )
            kept["gates"] = gates

        def cell_parts(group):
            if outside(group):
                return
            kept = kept_tiles[group]
            gate_i, gate_f, gate_g, gate_o = kept["gates"]
            old_part = work.tile([P, GROUP_COLS], F32)
            nc.gpsimd.tensor_tensor(out=old_part[:], in0=gate_f[:], in1=kept["hyper_c_t"], op=ALU.mult)
            new_part = work.tile([P, GROUP_COLS], F32)
            nc.gpsimd.tensor_tensor(out=new_part[:], in0=gate_i[:], in1=gate_g[:], op=ALU.mult)
            kept["old_part"] = old_part
            kept["new_part"] = new_part

        def cell_sum(group):
            if outside(group):
                return
            kept = kept_tiles[group]
            raw_c = work.tile([P, GROUP_COLS], F32)
            nc.vector.tensor_tensor(out=raw_c[:], in0=kept["old_part"][:], in1=kept["new_part"][:], op=ALU.add)
            kept["raw_c"] = raw_c

        def transpose_back(cell_group, gate_group):
            if outside(cell_group) and outside(gate_group):
                return
            back = psum.tile([P, 2, TILES_PER_GROUP, UNITS], F32, tag="back")
            for t in range(TILES_PER_GROUP):
                cols = slice(t * P, (t + 1) * P)
                if not outside(cell_group):
                    nc.tensor.transpose(back[:, 0, t, :], kept_tiles[cell_group]["raw_c"][:, cols], ident_f32[:])
                if not outside(gate_group):
                    nc.tensor.transpose(back[:, 1, t, :], kept_tiles[gate_group]["gates"][OUTPUT][:, cols], ident_f32[:])
            if not outside(cell_group):
                kept_tiles[cell_group]["raw_c_rows"] = back[:, 0, :, :]
            if not outside(gate_group):
                kept_tiles[gate_group]["gate_o_rows"] = back[:, 1, :, :]

        def cell_moments(group):
            if outside(group):
                return
            kept = kept_tiles[group]
            c_stats = work.tile([P, TILES_PER_GROUP, 6], F32)
            for t in range(TILES_PER_GROUP):
                nc.vector.bn_stats(out=c_stats[:, t, :], in_=kept["raw_c_rows"][:, t, :])
            kept["c_stats"] = c_stats

        def cell_centre(group):
            if outside(group):
                return
            kept = kept_tiles[group]
            c_mean_var = work.tile([P, TILES_PER_GROUP, 2], F32)
            for t in range(TILES_PER_GROUP):
                nc.vector.bn_aggr(out=c_mean_var[:, t, :], in_=kept["c_stats"][:, t, :])
            centred = work.tile([P, TILES_PER_GROUP, UNITS], F32, bufs=3)
            for t in range(TILES_PER_GROUP):
                nc.vector.scalar_tensor_tensor(
                    out=centred[:, t, :],
                    in0=kept["raw_c_rows"][:, t, :],
                    scalar=c_mean_var[:, t, 0:1],
                    in1=gamma_c_all,
                    op0=ALU.subtract,
                    op1=ALU.mult,
                )
            kept["c_mean_var"] = c_mean_var
            kept["centred"] = centred

        def cell_variance(group):
            if outside(group):
                return
            nc.vector.tensor_scalar_mul(
                out=shared_tiles[group + CELL_LAG]["moments"][:, GROUP_STATS:ROUND_STATS],
                in0=kept_tiles[group]["c_mean_var"][:, :, 1],
                scalar1=float(UNITS**3),
            )

        def cell_out(group):
            if outside(group):
                return
            kept = kept_tiles[group]
            new_c = work.tile([P, TILES_PER_GROUP, UNITS], F32, bufs=3)
            for t in range(TILES_PER_GROUP):
                nc.vector.scalar_tensor_tensor(
                    out=new_c[:, t, :],
                    in0=kept["centred"][:, t, :],
                    scalar=shared_tiles[group + CELL_LAG]["inv"][:, GROUP_STATS + t : GROUP_STATS + t + 1],
                    in1=beta_c_all,
                    op0=ALU.mult,
                    op1=ALU.add,
                )
            kept["new_c"] = new_c[:].rearrange("p t j -> p (t j)")
            nc.sync.dma_start(out=new_c_rows[:, group * GROUP_COLS : (group + 1) * GROUP_COLS], in_=kept["new_c"])

        def cell_tanh(group):
            if outside(group):
                return
            kept = kept_tiles[group]
            tanh_c = work.tile([P, GROUP_COLS], F32)
            nc.scalar.activation(out=tanh_c[:], in_=kept["new_c"], func=ACT.Tanh)
            kept["tanh_c"] = tanh_c

        def hidden_out(group):
            if outside(group):
                return
            kept = kept_tiles[group]
            new_h = work.tile([P, GROUP_COLS], F32, bufs=3)
            nc.vector.tensor_tensor(
                out=new_h[:],
                in0=kept["gate_o_rows"].rearrange("p t j -> p (t j)"),
                in1=kept["tanh_c"][:],
                op=ALU.mult,
            )
            nc.sync.dma_start(out=new_h_rows[:, group * GROUP_COLS : (group + 1) * GROUP_COLS], in_=new_h[:])

        with tc.manual_schedule():
            for i in range(-2, N_GROUPS + 6):
                load(i + 4)
                new_moments(i)
                activate(i - 2)
                add_bias(i, 0)
                plain_product(i, 1)
                cell_parts(i - 2)
                cell_moments(i - 3)
                hidden_out(i - 6)
                cell_tanh(i - 5)
                transpose_inputs(i + 2)
                add_products(i, 0)
                copy_inputs(i + 2)
                mx_product(i + 1, 0)
                add_bias(i, 1)
                plain_product(i + 1, 0)
                cell_centre(i - 3)
                sum_squares(i, 0)
                add_products(i, 1)
                mx_product(i + 1, 1)
                sum_squares(i, 1)
                cell_variance(i - 3)
                roots(i)
                std_eps(i - 1)
                quantise(i + 2)
                inv_std(i - 1)
                cell_sum(i - 2)
                transpose_back(i - 2, i - 5)
                gate_shift(i - 1)
                normalise_on_scalar(i - 1)
                cell_out(i - 4)
                normalise_on_vector(i - 1)
                transpose_normed(i - 1)
